import numpy as np
import ml_dtypes


def mxq(x, axis, fmt="e4m3"):
    dtype, down = {"e4m3": (ml_dtypes.float8_e4m3fn, 7), "e5m2": (ml_dtypes.float8_e5m2, 14)}[fmt]
    v = np.moveaxis(np.asarray(x, np.float32).astype(ml_dtypes.bfloat16).astype(np.float64), axis, -1)
    blocks = v.reshape(v.shape[:-1] + (-1, 32))
    amax = np.abs(blocks).max(-1, keepdims=True)
    byte = np.maximum(np.where(amax > 0, np.frexp(amax)[1] - 1 + 127, 0) - down, 1)
    scale = np.exp2(byte - 127.0)
    codes = (blocks / scale).astype(np.float32).astype(dtype).astype(np.float64)
    return np.moveaxis((codes * scale).reshape(v.shape), -1, axis)


WIDE = False


def mx_kscale(k):
    if not WIDE:
        return np.ones(k)
    levels = np.array([10, -10, 5, -5, 0])
    a = np.random.permutation(np.resize(levels, k // 512 * 4)).reshape(k // 512, 4)
    idx = np.arange(k)
    return np.exp2(a[idx // 512, idx % 128 // 32])


BF16 = ml_dtypes.bfloat16


def bf(x):
    return np.asarray(x, np.float32).astype(BF16)


def f64(x):
    return np.asarray(x).astype(np.float64)


E2M1 = np.array([0.0, 0.5, 1.0, 1.5, 2.0, 3.0, 4.0, 6.0, -0.0, -0.5, -1.0, -1.5, -2.0, -3.0, -4.0, -6.0])


def pack_weight(w, fmt):
    k, n = w.shape
    w = f64(bf(w)).reshape(k // 32, 32, n)
    amax = np.abs(w).max(1)
    if fmt == "e4m3":
        byte = np.frexp(amax)[1] - 1 + 127 - 7
    else:
        mant, ex = np.frexp(amax / 6.0)
        byte = np.where(mant > 0.5, ex, ex - 1) + 127
    byte = np.clip(np.where(amax > 0, byte, 1), 1, 254)
    scaled = (w * np.exp2(127.0 - byte)[:, None, :]).reshape(k, n).astype(np.float32)
    by_word = np.ascontiguousarray(scaled.reshape(k // 512, 128, 4, n).transpose(0, 1, 3, 2))
    if fmt == "e4m3":
        words = by_word.astype(ml_dtypes.float8_e4m3fn).view(np.uint8)
    else:
        c = by_word.astype(ml_dtypes.float4_e2m1fn).view(np.uint8) & 0xF
        words = c[..., 0::2] | (c[..., 1::2] << 4)
    return np.ascontiguousarray(words), np.ascontiguousarray(byte.astype(np.uint8).reshape(k // 512, 16, n))


def unpack_weight(words, scales, fmt):
    g, p, n, _ = words.shape
    if fmt == "e4m3":
        vals = np.ascontiguousarray(words).view(ml_dtypes.float8_e4m3fn).astype(np.float64)
    else:
        nib = np.empty((g, p, n, 4), np.uint8)
        nib[..., 0::2] = words & 0xF
        nib[..., 1::2] = words >> 4
        vals = E2M1[nib]
    vals = vals * np.repeat(np.exp2(scales.astype(np.float64) - 127.0), 8, axis=1)[..., None]
    return vals.transpose(0, 1, 3, 2).reshape(g * 512, n)


E, T, H, F = 2, 128, 2048, 2048


def gelu_tanh(v):
    return 0.5 * v * (1.0 + np.tanh(np.sqrt(2.0 / np.pi) * (v + 0.044715 * v**3)))


def setup_inputs():
    s, t = mx_kscale(H), mx_kscale(F)
    w1 = np.random.standard_normal((E, H, 2 * F)) / np.sqrt(H) / s[:, None]
    w1[:, :, F:] *= t
    w2 = np.random.standard_normal((E, F, H)) * 1.5 / np.sqrt(F) / t[:, None]
    weight2_words, weight2_scales = pack_weight(w2.reshape(E * F, H), "e4m3")
    return {"x": bf(np.random.standard_normal((E, T, H)) * s),
            "weight1": bf(w1.reshape(H, E * 2 * F)),
            "weight2_words": weight2_words,
            "weight2_scales": weight2_scales}


def reference(x, weight1, weight2_words, weight2_scales):
    w1 = f64(weight1).reshape(E, H, 2 * F)
    w2 = unpack_weight(weight2_words, weight2_scales, "e4m3").reshape(E, F, H)
    h = mxq(f64(x), 2, "e4m3") @ mxq(w1, 1, "e4m3")
    a, b = h[..., :F], h[..., F:]
    g = gelu_tanh(a) * b
    return mxq(g, 2, "e4m3") @ w2

@@ -1,0 +1,272 @@
+from contextlib import ExitStack
+
+import concourse.mybir as mybir
+from concourse.masks import make_identity
+
+FP8X4 = mybir.dt.float8_e4m3fn_x4
+BF16 = mybir.dt.bfloat16
+F32 = mybir.dt.float32
+I32 = mybir.dt.int32
+U32 = mybir.dt.uint32
+U8 = mybir.dt.uint8
+
+E, T, H, F = 2, 128, 2048, 2048
+P = 128
+FLOPS = 2 * E * T * H * 2 * F + 2 * E * T * F * H
+
+UNIT = 1024
+NU = 32
+SPLIT = [4, 2, 2, 2, 1, 1, 1, 1]
+VC = 488
+
+
+def tile_expert_w_kernel(tc, x, weight1, weight2_words, weight2_scales, out):
+    nc = tc.nc
+    gelu = mybir.ActivationFunctionType.Gelu_apprx_tanh
+    mult = mybir.AluOpType.mult
+    w1_rows = weight1.rearrange("r (h c) -> (r h) c", h=2)
+
+    with ExitStack() as ctx:
+        const = ctx.enter_context(tc.tile_pool(name="const", bufs=1))
+        stream = ctx.enter_context(tc.tile_pool(name="stream", bufs=4))
+        grp_pool = ctx.enter_context(tc.tile_pool(name="grp", bufs=3))
+        code_pool = ctx.enter_context(tc.tile_pool(name="code", bufs=5))
+        k4_pool = ctx.enter_context(tc.tile_pool(name="k4", bufs=2))
+        ga_pool = ctx.enter_context(tc.tile_pool(name="ga", bufs=4))
+        ost_pool = ctx.enter_context(tc.tile_pool(name="ost", bufs=4))
+        psum = ctx.enter_context(tc.psum_pool(name="psum", bufs=1))
+        ctx.enter_context(tc.manual_schedule())
+
+        ident_f = const.tile([P, P], F32, name="ident_f")
+        ident_b = const.tile([P, P], BF16, name="ident_b")
+        warm_in = const.tile([P, 8], F32, name="warm_in")
+        warm_out = const.tile([P, 8], F32, name="warm_out")
+        w2_planes = [const.tile([P, H], U8, name="w2_planes%d" % e, align_bytes=64) for e in range(E)]
+        xq = [const.tile([P, 4 * T], U32, name="xq%d" % e, align_bytes=64) for e in range(E)]
+        xs = [const.tile([P, 4 * T], U8, name="xs%d" % e, align_bytes=64) for e in range(E)]
+        gq = [const.tile([P, 4 * T], U32, name="gq%d" % e, align_bytes=64) for e in range(E)]
+        gs = [const.tile([P, 4 * T], U8, name="gs%d" % e, align_bytes=64) for e in range(E)]
+
+        chunk = {}
+        w2_words = {}
+        grouped = {}
+        codes = {}
+        planes = {}
+        hb = {}
+        xt = {}
+        xg = {}
+        ga = {}
+        gp = {}
+        pt = {}
+        gg_t = {}
+
+        def load_chunk(k):
+            nblk = SPLIT[k]
+            wdt = 2 * F // nblk
+            t = stream.tile([P, nblk, 4, wdt], BF16, tag="stream", name="w1c%d" % k, align_bytes=64)
+            chunk[k] = t
+            for b in range(nblk):
+                nc.sync.dma_start(
+                    out=t[:, b, :, :],
+                    in_=w1_rows[512 * k : 512 * (k + 1), wdt * b : wdt * (b + 1)].rearrange("(p j) w -> p j w", j=4),
+                )
+
+        def load_w2(e):
+            t = stream.tile([P, 4, H], I32, tag="stream", name="w2w%d" % e, align_bytes=64)
+            w2_words[e] = t
+            for g in range(4):
+                nc.sync.dma_start(
+                    out=t[:, g, :],
+                    in_=weight2_words[4 * e + g].rearrange("p n t -> p (n t)").bitcast(I32),
+                )
+
+        def load_next(k):
+            if k < 8:
+                load_chunk(k)
+            elif k < 10:
+                load_w2(k - 8)
+
+        def unit_src(u, lo, hi):
+            k, q = divmod(u, 4)
+            per = 4 // SPLIT[k]
+            off = (q % per) * UNIT
+            return chunk[k][:, q // per, :, off + lo : off + hi].rearrange("p t (c i) -> p c t i", i=4)
+
+        def regroup(u):
+            g = grp_pool.tile([P, UNIT, 4], BF16, tag="grp", name="grp%d" % u, align_bytes=64)
+            grouped[u] = g
+            nc.vector.tensor_copy(
+                out=g[:, 0:VC, :].rearrange("p (c i) t -> p c t i", i=4), in_=unit_src(u, 0, VC)
+            )
+            nc.scalar.copy(
+                out=g[:, VC:UNIT, :].rearrange("p (c i) t -> p c t i", i=4), in_=unit_src(u, VC, UNIT)
+            )
+            if u % 4 == 3:
+                load_next(u // 4 + 4)
+
+        def quant(u):
+            cw = code_pool.tile([P, UNIT], U32, tag="codes", name="codes%d" % u, align_bytes=64)
+            pl = code_pool.tile([P, UNIT], U8, tag="planes", name="planes%d" % u, align_bytes=64)
+            codes[u] = cw
+            planes[u] = pl
+            nc.vector.quantize_mx(
+                out=cw[:].bitcast(FP8X4), scales=pl[:], in_=grouped[u][:].rearrange("p w t -> p (w t)")
+            )
+
+        def passes(u):
+            k, q = divmod(u, 4)
+            e, c = divmod(k, 4)
+            for half in range(2):
+                bank = 2 * q + half
+                if c == 0:
+                    hb[bank] = psum.tile([P, 512], F32, tag="b%d" % bank, name="h%d_%d" % (e, bank))
+                cols = slice(512 * half, 512 * (half + 1))
+                nc.tensor.matmul_mx(
+                    out=hb[bank][:],
+                    lhsT=xq[e][:, T * c : T * (c + 1)].bitcast(FP8X4),
+                    lhsT_scale=xs[e][:, T * c : T * (c + 1)],
+                    rhs=codes[u][:, cols].bitcast(FP8X4),
+                    rhs_scale=planes[u][:, cols],
+                    start=(c == 0),
+                    stop=(c == 3),
+                )
+
+        def xcopy(e):
+            t = k4_pool.tile([P, 4, T, 4], BF16, tag="k4", name="xg%d" % e, align_bytes=64)
+            xg[e] = t
+            words = t[:].bitcast(F32)
+            nc.vector.tensor_copy(out=words[:, 0:2, :, :], in_=xt[(e, 0)][:].rearrange("p c u k -> p c k u"))
+            nc.scalar.copy(out=words[:, 2:4, :, :], in_=xt[(e, 1)][:].rearrange("p c u k -> p c k u"))
+
+        def xquant(e):
+            nc.vector.quantize_mx(
+                out=xq[e][:].bitcast(FP8X4), scales=xs[e][:], in_=xg[e][:].rearrange("p c k t -> p (c k t)")
+            )
+
+        def gelu_a(e, i):
+            t = ga_pool.tile([P, 512], F32, tag="ga", name="ga%d_%d" % (e, i))
+            ga[i] = t
+            nc.scalar.activation(out=t[:], in_=hb[i][:], func=gelu)
+
+        def gate(e, i):
+            if i == 0:
+                gp[e] = k4_pool.tile([P, 4, 4, P], BF16, tag="k4", name="gp%d" % e, align_bytes=64)
+            nc.vector.tensor_tensor(
+                out=gp[e][:, i, :, :],
+                in0=hb[4 + i][:].rearrange("k (p t) -> k t p", t=4),
+                in1=ga[i][:].rearrange("k (p t) -> k t p", t=4),
+                op=mult,
+            )
+
+        def g_transpose(e, i):
+            t = psum.tile([P, 4, T], BF16, tag="b%d" % (4 + i), name="pt%d_%d" % (e, i))
+            pt[i] = t
+            for tt in range(4):
+                nc.tensor.transpose(t[:, tt, :], gp[e][:, i, tt, :], ident_b[:])
+
+        def g_copy(e, i):
+            if i == 0:
+                gg_t[e] = k4_pool.tile([P, 4, T, 4], BF16, tag="k4", name="gg%d" % e, align_bytes=64)
+            src = pt[i][:].rearrange("p t k -> p k t")
+            if i % 2 == 0:
+                nc.vector.tensor_copy(out=gg_t[e][:, i, :, :], in_=src)
+            else:
+                nc.scalar.copy(out=gg_t[e][:, i, :, :], in_=src)
+
+        def g_quant(e):
+            nc.vector.quantize_mx(
+                out=gq[e][:].bitcast(FP8X4), scales=gs[e][:], in_=gg_t[e][:].rearrange("p i k t -> p (i k t)")
+            )
+
+        for e in range(E):
+            nc.vector.memset(w2_planes[e][:].bitcast(I32), 0)
+        nc.vector.memset(warm_in[:], 0.0)
+        nc.scalar.activation(out=warm_out[:], in_=warm_in[:], func=gelu)
+        make_identity(nc, ident_f[:])
+        for e in range(E):
+            for quad in range(4):
+                nc.gpsimd.dma_start(
+                    out=w2_planes[e][32 * quad : 32 * quad + 16, :].bitcast(F32),
+                    in_=weight2_scales[4 * e : 4 * e + 4, 4 * quad : 4 * quad + 4, :].bitcast(F32),
+                )
+        make_identity(nc, ident_b[:])
+
+        xr = stream.tile([P, E, H], BF16, tag="stream", name="xr", align_bytes=64)
+        nc.sync.dma_start(out=xr[:], in_=x.rearrange("e t h -> t e h"))
+        for k in range(3):
+            load_chunk(k)
+        xw = xr[:].bitcast(F32)
+        for e in range(E):
+            for half in range(2):
+                t = psum.tile([P, 2, 2, T], F32, tag="b%d" % (4 + 2 * e + half), name="xt%d_%d" % (e, half))
+                xt[(e, half)] = t
+                for cc in range(2):
+                    c = 2 * half + cc
+                    for u in range(2):
+                        nc.tensor.transpose(t[:, cc, u, :], xw[:, e, 256 * c + u : 256 * (c + 1) : 2], ident_f[:])
+        load_chunk(3)
+
+        xcopy(0)
+        regroup(0)
+        xquant(0)
+        xcopy(1)
+
+        for u in range(NU + 3):
+            if u + 1 < NU:
+                regroup(u + 1)
+            if u == 0:
+                xquant(1)
+            e, r = divmod(u - 16, 16) if u >= 16 else (0, -1)
+            if r == 0:
+                gate(e, 2)
+                gate(e, 3)
+                for i in range(4):
+                    g_transpose(e, i)
+            if r == 1:
+                for i in range(4):
+                    g_copy(e, i)
+            if r == 2:
+                g_quant(e)
+            if u < NU:
+                quant(u)
+                passes(u)
+            e, r = divmod(u, 16)
+            if r == 13:
+                gelu_a(e, 0)
+                gelu_a(e, 1)
+            if r == 14:
+                gelu_a(e, 2)
+                gelu_a(e, 3)
+            if r == 15:
+                gate(e, 0)
+                gate(e, 1)
+
+        def pass2(e, acc, nb, g):
+            cols = slice(512 * nb, 512 * (nb + 1))
+            nc.tensor.matmul_mx(
+                out=acc[:],
+                lhsT=gq[e][:, T * g : T * (g + 1)].bitcast(FP8X4),
+                lhsT_scale=gs[e][:, T * g : T * (g + 1)],
+                rhs=w2_words[e][:, g, cols].bitcast(FP8X4),
+                rhs_scale=w2_planes[e][4 * g : P, cols],
+                start=(g == 0),
+                stop=(g == 3),
+            )
+
+        def drain(e, accs):
+            for h in range(2):
+                st = ost_pool.tile([P, 1024], F32, tag="ost", name="ost%d_%d" % (e, h))
+                nc.vector.tensor_copy(out=st[:, 0:512], in_=accs[2 * h][:])
+                nc.scalar.copy(out=st[:, 512:1024], in_=accs[2 * h + 1][:])
+                nc.sync.dma_start(out=out[e][:, 1024 * h : 1024 * (h + 1)], in_=st[:])
+
+        acc0 = [psum.tile([P, 512], F32, tag="b%d" % nb, name="o0_%d" % nb) for nb in range(4)]
+        for nb in range(4):
+            for g in range(4):
+                pass2(0, acc0[nb], nb, g)
+        drain(0, acc0)
+        acc1 = [psum.tile([P, 512], F32, tag="b%d" % (4 + nb), name="o1_%d" % nb) for nb in range(4)]
+        for g in range(4):
+            for nb in range(4):
+                pass2(1, acc1[nb], nb, g)
+        drain(1, acc1)

@@ -15,9 +15,11 @@ P = 128
 FLOPS = 2 * E * T * H * 2 * F + 2 * E * T * F * H
 
 UNIT = 1024
-NU = 32
-SPLIT = [4, 2, 2, 2, 1, 1, 1, 1]
+SPLIT = [4, 2, 2, 2, 2, 1, 1, 1]
 VC = 488
+VC_LAST = {}
+ORDER = [(k, q) for k in range(8) for q in ((0, 2, 1, 3) if k == 7 else (0, 1, 2, 3))]
+NU = len(ORDER)
 
 
 def tile_expert_w_kernel(tc, x, weight1, weight2_words, weight2_scales, out):
@@ -59,17 +61,37 @@ def tile_expert_w_kernel(tc, x, weight1, weight2_words, weight2_scales, out):
         gp = {}
         pt = {}
         gg_t = {}
+        acc = {}
+        ost = {}
+        scale_loads = []
+
+        def load_scales():
+            if len(scale_loads) < 4 * E:
+                e, quad = divmod(len(scale_loads), 4)
+                scale_loads.append(quad)
+                nc.sync.dma_start(
+                    out=w2_planes[e][32 * quad : 32 * quad + 16, :].bitcast(I32),
+                    in_=weight2_scales[4 * e : 4 * e + 4, 4 * quad : 4 * quad + 4, :].bitcast(I32),
+                )
+
+        def alloc_chunk(k):
+            nblk = SPLIT[k]
+            chunk[k] = stream.tile(
+                [P, nblk, 4, 2 * F // nblk], BF16, tag="stream", name="w1c%d" % k, align_bytes=64
+            )
+
+        def load_block(k, b):
+            wdt = 2 * F // SPLIT[k]
+            nc.sync.dma_start(
+                out=chunk[k][:, b, :, :],
+                in_=w1_rows[512 * k : 512 * (k + 1), wdt * b : wdt * (b + 1)].rearrange("(p j) w -> p j w", j=4),
+            )
 
         def load_chunk(k):
-            nblk = SPLIT[k]
-            wdt = 2 * F // nblk
-            t = stream.tile([P, nblk, 4, wdt], BF16, tag="stream", name="w1c%d" % k, align_bytes=64)
-            chunk[k] = t
-            for b in range(nblk):
-                nc.sync.dma_start(
-                    out=t[:, b, :, :],
-                    in_=w1_rows[512 * k : 512 * (k + 1), wdt * b : wdt * (b + 1)].rearrange("(p j) w -> p j w", j=4),
-                )
+            alloc_chunk(k)
+            for b in range(SPLIT[k]):
+                load_block(k, b)
+                load_scales()
 
         def load_w2(e):
             t = stream.tile([P, 4, H], I32, tag="stream", name="w2w%d" % e, align_bytes=64)
@@ -86,35 +108,36 @@ def tile_expert_w_kernel(tc, x, weight1, weight2_words, weight2_scales, out):
             elif k < 10:
                 load_w2(k - 8)
 
-        def unit_src(u, lo, hi):
-            k, q = divmod(u, 4)
+        def unit_src(n, lo, hi):
+            k, q = ORDER[n]
             per = 4 // SPLIT[k]
             off = (q % per) * UNIT
             return chunk[k][:, q // per, :, off + lo : off + hi].rearrange("p t (c i) -> p c t i", i=4)
 
-        def regroup(u):
-            g = grp_pool.tile([P, UNIT, 4], BF16, tag="grp", name="grp%d" % u, align_bytes=64)
-            grouped[u] = g
+        def regroup(n):
+            g = grp_pool.tile([P, UNIT, 4], BF16, tag="grp", name="grp%d" % n, align_bytes=64)
+            grouped[n] = g
+            vc = VC_LAST.get(n, VC)
             nc.vector.tensor_copy(
-                out=g[:, 0:VC, :].rearrange("p (c i) t -> p c t i", i=4), in_=unit_src(u, 0, VC)
+                out=g[:, 0:vc, :].rearrange("p (c i) t -> p c t i", i=4), in_=unit_src(n, 0, vc)
             )
             nc.scalar.copy(
-                out=g[:, VC:UNIT, :].rearrange("p (c i) t -> p c t i", i=4), in_=unit_src(u, VC, UNIT)
+                out=g[:, vc:UNIT, :].rearrange("p (c i) t -> p c t i", i=4), in_=unit_src(n, vc, UNIT)
             )
-            if u % 4 == 3:
-                load_next(u // 4 + 4)
+            if n % 4 == 3:
+                load_next(n // 4 + 4)
 
-        def quant(u):
-            cw = code_pool.tile([P, UNIT], U32, tag="codes", name="codes%d" % u, align_bytes=64)
-            pl = code_pool.tile([P, UNIT], U8, tag="planes", name="planes%d" % u, align_bytes=64)
-            codes[u] = cw
-            planes[u] = pl
+        def quant(n):
+            cw = code_pool.tile([P, UNIT], U32, tag="codes", name="codes%d" % n, align_bytes=64)
+            pl = code_pool.tile([P, UNIT], U8, tag="planes", name="planes%d" % n, align_bytes=64)
+            codes[n] = cw
+            planes[n] = pl
             nc.vector.quantize_mx(
-                out=cw[:].bitcast(FP8X4), scales=pl[:], in_=grouped[u][:].rearrange("p w t -> p (w t)")
+                out=cw[:].bitcast(FP8X4), scales=pl[:], in_=grouped[n][:].rearrange("p w t -> p (w t)")
             )
 
-        def passes(u):
-            k, q = divmod(u, 4)
+        def passes(n):
+            k, q = ORDER[n]
             e, c = divmod(k, 4)
             for half in range(2):
                 bank = 2 * q + half
@@ -125,8 +148,8 @@ def tile_expert_w_kernel(tc, x, weight1, weight2_words, weight2_scales, out):
                     out=hb[bank][:],
                     lhsT=xq[e][:, T * c : T * (c + 1)].bitcast(FP8X4),
                     lhsT_scale=xs[e][:, T * c : T * (c + 1)],
-                    rhs=codes[u][:, cols].bitcast(FP8X4),
-                    rhs_scale=planes[u][:, cols],
+                    rhs=codes[n][:, cols].bitcast(FP8X4),
+                    rhs_scale=planes[n][:, cols],
                     start=(c == 0),
                     stop=(c == 3),
                 )
@@ -173,28 +196,57 @@ def tile_expert_w_kernel(tc, x, weight1, weight2_words, weight2_scales, out):
             else:
                 nc.scalar.copy(out=gg_t[e][:, i, :, :], in_=src)
 
-        def g_quant(e):
+        def g_quant(e, lo, hi):
             nc.vector.quantize_mx(
-                out=gq[e][:].bitcast(FP8X4), scales=gs[e][:], in_=gg_t[e][:].rearrange("p i k t -> p (i k t)")
+                out=gq[e][:, T * lo : T * hi].bitcast(FP8X4),
+                scales=gs[e][:, T * lo : T * hi],
+                in_=gg_t[e][:, lo:hi, :, :].rearrange("p i k t -> p (i k t)"),
             )
+
+        def pass2(e, nb, g, bank):
+            if g == 0:
+                acc[(e, nb)] = psum.tile([P, 512], F32, tag="b%d" % bank, name="o%d_%d" % (e, nb))
+            cols = slice(512 * nb, 512 * (nb + 1))
+            nc.tensor.matmul_mx(
+                out=acc[(e, nb)][:],
+                lhsT=gq[e][:, T * g : T * (g + 1)].bitcast(FP8X4),
+                lhsT_scale=gs[e][:, T * g : T * (g + 1)],
+                rhs=w2_words[e][:, g, cols].bitcast(FP8X4),
+                rhs_scale=w2_planes[e][4 * g : P, cols],
+                start=(g == 0),
+                stop=(g == 3),
+            )
+
+        def drain(e, nb, on_vector):
+            if nb % 2 == 0:
+                ost[e] = ost_pool.tile([P, 1024], F32, tag="ost", name="ost%d_%d" % (e, nb))
+            dst = ost[e][:, 512 * (nb % 2) : 512 * (nb % 2 + 1)]
+            if on_vector:
+                nc.vector.tensor_copy(out=dst, in_=acc[(e, nb)][:])
+            else:
+                nc.scalar.copy(out=dst, in_=acc[(e, nb)][:])
+            if nb % 2 == 1:
+                nc.sync.dma_start(out=out[e][:, 512 * (nb - 1) : 512 * (nb + 1)], in_=ost[e][:])
 
         for e in range(E):
             nc.vector.memset(w2_planes[e][:].bitcast(I32), 0)
         nc.vector.memset(warm_in[:], 0.0)
         nc.scalar.activation(out=warm_out[:], in_=warm_in[:], func=gelu)
         make_identity(nc, ident_f[:])
-        for e in range(E):
-            for quad in range(4):
-                nc.gpsimd.dma_start(
-                    out=w2_planes[e][32 * quad : 32 * quad + 16, :].bitcast(F32),
-                    in_=weight2_scales[4 * e : 4 * e + 4, 4 * quad : 4 * quad + 4, :].bitcast(F32),
-                )
         make_identity(nc, ident_b[:])
 
+        alloc_chunk(0)
+        load_block(0, 0)
         xr = stream.tile([P, E, H], BF16, tag="stream", name="xr", align_bytes=64)
         nc.sync.dma_start(out=xr[:], in_=x.rearrange("e t h -> t e h"))
-        for k in range(3):
-            load_chunk(k)
+        for b in range(1, SPLIT[0]):
+            load_block(0, b)
+            load_scales()
+        load_chunk(1)
+        load_chunk(2)
+
+        regroup(0)
+        quant(0)
         xw = xr[:].bitcast(F32)
         for e in range(E):
             for half in range(2):
@@ -205,68 +257,76 @@ def tile_expert_w_kernel(tc, x, weight1, weight2_words, weight2_scales, out):
                     for u in range(2):
                         nc.tensor.transpose(t[:, cc, u, :], xw[:, e, 256 * c + u : 256 * (c + 1) : 2], ident_f[:])
         load_chunk(3)
-
         xcopy(0)
-        regroup(0)
-        xquant(0)
         xcopy(1)
+        xquant(0)
+        regroup(1)
+        xquant(1)
+        passes(0)
 
-        for u in range(NU + 3):
-            if u + 1 < NU:
-                regroup(u + 1)
-            if u == 0:
-                xquant(1)
-            e, r = divmod(u - 16, 16) if u >= 16 else (0, -1)
-            if r == 0:
-                gate(e, 2)
-                gate(e, 3)
+        for n in range(1, NU):
+            if n + 1 < NU:
+                regroup(n + 1)
+            if n == 16:
+                gate(0, 2)
+                gate(0, 3)
                 for i in range(4):
-                    g_transpose(e, i)
-            if r == 1:
+                    g_transpose(0, i)
+            if n == 17:
                 for i in range(4):
-                    g_copy(e, i)
-            if r == 2:
-                g_quant(e)
-            if u < NU:
-                quant(u)
-                passes(u)
-            e, r = divmod(u, 16)
-            if r == 13:
-                gelu_a(e, 0)
-                gelu_a(e, 1)
-            if r == 14:
-                gelu_a(e, 2)
-                gelu_a(e, 3)
-            if r == 15:
-                gate(e, 0)
-                gate(e, 1)
+                    g_copy(0, i)
+            if n == 18:
+                g_quant(0, 0, 4)
+            if n == 30:
+                gate(1, 0)
+                gate(1, 1)
+                g_transpose(1, 0)
+                g_transpose(1, 1)
+            if n == 31:
+                g_copy(1, 0)
+                g_copy(1, 1)
+            quant(n)
+            passes(n)
+            if n == 13:
+                gelu_a(0, 0)
+                gelu_a(0, 1)
+            if n == 14:
+                gelu_a(0, 2)
+                gelu_a(0, 3)
+            if n == 15:
+                gate(0, 0)
+                gate(0, 1)
+            if n == 29:
+                gelu_a(1, 0)
+                gelu_a(1, 1)
+            if n == 30:
+                for nb in range(2):
+                    for g in range(4):
+                        pass2(0, nb, g, nb)
 
-        def pass2(e, acc, nb, g):
-            cols = slice(512 * nb, 512 * (nb + 1))
-            nc.tensor.matmul_mx(
-                out=acc[:],
-                lhsT=gq[e][:, T * g : T * (g + 1)].bitcast(FP8X4),
-                lhsT_scale=gs[e][:, T * g : T * (g + 1)],
-                rhs=w2_words[e][:, g, cols].bitcast(FP8X4),
-                rhs_scale=w2_planes[e][4 * g : P, cols],
-                start=(g == 0),
-                stop=(g == 3),
-            )
-
-        def drain(e, accs):
-            for h in range(2):
-                st = ost_pool.tile([P, 1024], F32, tag="ost", name="ost%d_%d" % (e, h))
-                nc.vector.tensor_copy(out=st[:, 0:512], in_=accs[2 * h][:])
-                nc.scalar.copy(out=st[:, 512:1024], in_=accs[2 * h + 1][:])
-                nc.sync.dma_start(out=out[e][:, 1024 * h : 1024 * (h + 1)], in_=st[:])
-
-        acc0 = [psum.tile([P, 512], F32, tag="b%d" % nb, name="o0_%d" % nb) for nb in range(4)]
-        for nb in range(4):
+        gelu_a(1, 2)
+        gelu_a(1, 3)
+        g_quant(1, 0, 2)
+        for nb in range(2, 4):
             for g in range(4):
-                pass2(0, acc0[nb], nb, g)
-        drain(0, acc0)
-        acc1 = [psum.tile([P, 512], F32, tag="b%d" % (4 + nb), name="o1_%d" % nb) for nb in range(4)]
-        for g in range(4):
+                pass2(0, nb, g, nb + 2)
+        drain(0, 0, False)
+        drain(0, 1, False)
+        gate(1, 2)
+        gate(1, 3)
+        g_transpose(1, 2)
+        g_transpose(1, 3)
+        bank1 = [2, 3, 0, 1]
+        for g in range(2):
             for nb in range(4):
-                pass2(1, acc1[nb], nb, g)
-        drain(1, acc1)
+                pass2(1, nb, g, bank1[nb])
+        g_copy(1, 2)
+        g_copy(1, 3)
+        g_quant(1, 2, 4)
+        drain(0, 2, False)
+        drain(0, 3, False)
+        for g in range(2, 4):
+            for nb in range(4):
+                pass2(1, nb, g, bank1[nb])
+        for nb in range(4):
+            drain(1, nb, nb % 2 == 0)

@@ -16,7 +16,7 @@ FLOPS = 2 * E * T * H * 2 * F + 2 * E * T * F * H
 
 UNIT = 1024
 SPLIT = [4, 2, 2, 2, 2, 1, 1, 1]
-VC = 488
+VC = 512
 VC_LAST = {}
 ORDER = [(k, q) for k in range(8) for q in ((0, 2, 1, 3) if k == 7 else (0, 1, 2, 3))]
 NU = len(ORDER)

@@ -15,8 +15,8 @@ P = 128
 FLOPS = 2 * E * T * H * 2 * F + 2 * E * T * F * H
 
 UNIT = 1024
-SPLIT = [4, 2, 2, 2, 2, 1, 1, 1]
-VC = 512
+SPLIT = [4, 1, 1, 1, 1, 1, 1, 1]
+VC = 488
 VC_LAST = {}
 ORDER = [(k, q) for k in range(8) for q in ((0, 2, 1, 3) if k == 7 else (0, 1, 2, 3))]
 NU = len(ORDER)

@@ -12,14 +12,21 @@ U8 = mybir.dt.uint8
 
 E, T, H, F = 2, 128, 2048, 2048
 P = 128
+PACK = 4
+K_PASS = P * PACK
+PASSES = H // K_PASS
+BANK = 512
+UNIT = 2 * BANK
+UNITS = 2 * F // UNIT
+CHUNKS = E * PASSES
+SLOTS = 4
 FLOPS = 2 * E * T * H * 2 * F + 2 * E * T * F * H
 
-UNIT = 1024
-SPLIT = [4, 1, 1, 1, 1, 1, 1, 1]
-VC = 488
-VC_LAST = {}
-ORDER = [(k, q) for k in range(8) for q in ((0, 2, 1, 3) if k == 7 else (0, 1, 2, 3))]
-NU = len(ORDER)
+PIECES = [4, 2, 2, 2, 2, 1, 1, 1]
+VECTOR_COLS = 488
+ORDER = [(k, u) for k in range(CHUNKS - 1) for u in range(UNITS)] + [(CHUNKS - 1, u) for u in (0, 2, 1, 3)]
+CLOSES = dict(((e, u), ORDER.index((PASSES * e + PASSES - 1, u))) for e in range(E) for u in range(UNITS))
+OUT_BANKS = [[0, 1, 4, 5], [2, 3, 0, 1]]
 
 
 def tile_expert_w_kernel(tc, x, weight1, weight2_words, weight2_scales, out):
@@ -30,303 +37,264 @@ def tile_expert_w_kernel(tc, x, weight1, weight2_words, weight2_scales, out):
 
     with ExitStack() as ctx:
         const = ctx.enter_context(tc.tile_pool(name="const", bufs=1))
-        stream = ctx.enter_context(tc.tile_pool(name="stream", bufs=4))
-        grp_pool = ctx.enter_context(tc.tile_pool(name="grp", bufs=3))
-        code_pool = ctx.enter_context(tc.tile_pool(name="code", bufs=5))
-        k4_pool = ctx.enter_context(tc.tile_pool(name="k4", bufs=2))
-        ga_pool = ctx.enter_context(tc.tile_pool(name="ga", bufs=4))
-        ost_pool = ctx.enter_context(tc.tile_pool(name="ost", bufs=4))
+        stream = ctx.enter_context(tc.tile_pool(name="stream", bufs=SLOTS))
+        regrouped = ctx.enter_context(tc.tile_pool(name="regrouped", bufs=3))
+        quantised = ctx.enter_context(tc.tile_pool(name="quantised", bufs=5))
+        small = ctx.enter_context(tc.tile_pool(name="small", bufs=2))
+        gelu_pool = ctx.enter_context(tc.tile_pool(name="gelu", bufs=4))
+        store_pool = ctx.enter_context(tc.tile_pool(name="store", bufs=4))
         psum = ctx.enter_context(tc.psum_pool(name="psum", bufs=1))
         ctx.enter_context(tc.manual_schedule())
 
-        ident_f = const.tile([P, P], F32, name="ident_f")
-        ident_b = const.tile([P, P], BF16, name="ident_b")
+        ident_f32 = const.tile([P, P], F32, name="ident_f32")
+        ident_bf16 = const.tile([P, P], BF16, name="ident_bf16")
         warm_in = const.tile([P, 8], F32, name="warm_in")
         warm_out = const.tile([P, 8], F32, name="warm_out")
         w2_planes = [const.tile([P, H], U8, name="w2_planes%d" % e, align_bytes=64) for e in range(E)]
-        xq = [const.tile([P, 4 * T], U32, name="xq%d" % e, align_bytes=64) for e in range(E)]
-        xs = [const.tile([P, 4 * T], U8, name="xs%d" % e, align_bytes=64) for e in range(E)]
-        gq = [const.tile([P, 4 * T], U32, name="gq%d" % e, align_bytes=64) for e in range(E)]
-        gs = [const.tile([P, 4 * T], U8, name="gs%d" % e, align_bytes=64) for e in range(E)]
+        x_words = [const.tile([P, PASSES * T], U32, name="x_words%d" % e, align_bytes=64) for e in range(E)]
+        x_planes = [const.tile([P, PASSES * T], U8, name="x_planes%d" % e, align_bytes=64) for e in range(E)]
+        g_words = [const.tile([P, PASSES * T], U32, name="g_words%d" % e, align_bytes=64) for e in range(E)]
+        g_planes = [const.tile([P, PASSES * T], U8, name="g_planes%d" % e, align_bytes=64) for e in range(E)]
 
         chunk = {}
         w2_words = {}
-        grouped = {}
-        codes = {}
-        planes = {}
-        hb = {}
-        xt = {}
-        xg = {}
-        ga = {}
-        gp = {}
-        pt = {}
-        gg_t = {}
+        unit_bf16 = {}
+        unit_words = {}
+        unit_planes = {}
+        bank = {}
+        x_t = {}
+        x_bf16 = {}
+        gelu_a = {}
+        g_sorted = {}
+        g_t = {}
+        g_bf16 = {}
         acc = {}
-        ost = {}
-        scale_loads = []
+        staged = {}
 
-        def load_scales():
-            if len(scale_loads) < 4 * E:
-                e, quad = divmod(len(scale_loads), 4)
-                scale_loads.append(quad)
-                nc.sync.dma_start(
-                    out=w2_planes[e][32 * quad : 32 * quad + 16, :].bitcast(I32),
-                    in_=weight2_scales[4 * e : 4 * e + 4, 4 * quad : 4 * quad + 4, :].bitcast(I32),
-                )
-
-        def alloc_chunk(k):
-            nblk = SPLIT[k]
-            chunk[k] = stream.tile(
-                [P, nblk, 4, 2 * F // nblk], BF16, tag="stream", name="w1c%d" % k, align_bytes=64
-            )
-
-        def load_block(k, b):
-            wdt = 2 * F // SPLIT[k]
+        def load_piece(k, piece):
+            width = 2 * F // PIECES[k]
             nc.sync.dma_start(
-                out=chunk[k][:, b, :, :],
-                in_=w1_rows[512 * k : 512 * (k + 1), wdt * b : wdt * (b + 1)].rearrange("(p j) w -> p j w", j=4),
+                out=chunk[k][:, piece, :, :],
+                in_=w1_rows[K_PASS * k : K_PASS * (k + 1), width * piece : width * (piece + 1)].rearrange(
+                    "(p j) w -> p j w", j=PACK
+                ),
             )
 
-        def load_chunk(k):
-            alloc_chunk(k)
-            for b in range(SPLIT[k]):
-                load_block(k, b)
-                load_scales()
+        def load_scale_rows(e, quadrant):
+            nc.sync.dma_start(
+                out=w2_planes[e][32 * quadrant : 32 * quadrant + 16, :].bitcast(I32),
+                in_=weight2_scales[PASSES * e : PASSES * (e + 1), 4 * quadrant : 4 * quadrant + 4, :].bitcast(I32),
+            )
 
-        def load_w2(e):
-            t = stream.tile([P, 4, H], I32, tag="stream", name="w2w%d" % e, align_bytes=64)
-            w2_words[e] = t
-            for g in range(4):
-                nc.sync.dma_start(
-                    out=t[:, g, :],
-                    in_=weight2_words[4 * e + g].rearrange("p n t -> p (n t)").bitcast(I32),
-                )
+        def new_chunk(k):
+            chunk[k] = stream.tile(
+                [P, PIECES[k], PACK, 2 * F // PIECES[k]], BF16, tag="stream", name="chunk%d" % k, align_bytes=64
+            )
 
-        def load_next(k):
-            if k < 8:
-                load_chunk(k)
-            elif k < 10:
-                load_w2(k - 8)
-
-        def unit_src(n, lo, hi):
-            k, q = ORDER[n]
-            per = 4 // SPLIT[k]
-            off = (q % per) * UNIT
-            return chunk[k][:, q // per, :, off + lo : off + hi].rearrange("p t (c i) -> p c t i", i=4)
+        def load_stream(i):
+            if i < CHUNKS:
+                new_chunk(i)
+                for piece in range(PIECES[i]):
+                    load_piece(i, piece)
+                if i >= PASSES:
+                    for quadrant in (2 * (i % 2), 2 * (i % 2) + 1):
+                        load_scale_rows((i - PASSES) // 2, quadrant)
+            elif i < CHUNKS + E:
+                e = i - CHUNKS
+                w2_words[e] = stream.tile([P, PASSES, H], I32, tag="stream", name="w2_words%d" % e, align_bytes=64)
+                for c in range(PASSES):
+                    nc.sync.dma_start(
+                        out=w2_words[e][:, c, :],
+                        in_=weight2_words[PASSES * e + c].rearrange("p n t -> p (n t)").bitcast(I32),
+                    )
 
         def regroup(n):
-            g = grp_pool.tile([P, UNIT, 4], BF16, tag="grp", name="grp%d" % n, align_bytes=64)
-            grouped[n] = g
-            vc = VC_LAST.get(n, VC)
-            nc.vector.tensor_copy(
-                out=g[:, 0:vc, :].rearrange("p (c i) t -> p c t i", i=4), in_=unit_src(n, 0, vc)
-            )
-            nc.scalar.copy(
-                out=g[:, vc:UNIT, :].rearrange("p (c i) t -> p c t i", i=4), in_=unit_src(n, vc, UNIT)
-            )
-            if n % 4 == 3:
-                load_next(n // 4 + 4)
+            k, u = ORDER[n]
+            per_piece = UNITS // PIECES[k]
+            first = (u % per_piece) * UNIT
+            rows = chunk[k][:, u // per_piece, :, first : first + UNIT]
+            unit_bf16[n] = regrouped.tile([P, UNIT, PACK], BF16, tag="unit", name="unit%d" % n, align_bytes=64)
+            for copy, cols in (
+                (nc.vector.tensor_copy, slice(0, VECTOR_COLS)),
+                (nc.scalar.copy, slice(VECTOR_COLS, UNIT)),
+            ):
+                copy(
+                    out=unit_bf16[n][:, cols, :].rearrange("p (c i) j -> p c j i", i=4),
+                    in_=rows[:, :, cols].rearrange("p j (c i) -> p c j i", i=4),
+                )
+            if n % UNITS == UNITS - 1:
+                load_stream(n // UNITS + SLOTS)
 
-        def quant(n):
-            cw = code_pool.tile([P, UNIT], U32, tag="codes", name="codes%d" % n, align_bytes=64)
-            pl = code_pool.tile([P, UNIT], U8, tag="planes", name="planes%d" % n, align_bytes=64)
-            codes[n] = cw
-            planes[n] = pl
+        def quantise(n):
+            unit_words[n] = quantised.tile([P, UNIT], U32, tag="words", name="words%d" % n, align_bytes=64)
+            unit_planes[n] = quantised.tile([P, UNIT], U8, tag="planes", name="planes%d" % n, align_bytes=64)
             nc.vector.quantize_mx(
-                out=cw[:].bitcast(FP8X4), scales=pl[:], in_=grouped[n][:].rearrange("p w t -> p (w t)")
+                out=unit_words[n][:].bitcast(FP8X4),
+                scales=unit_planes[n][:],
+                in_=unit_bf16[n][:].rearrange("p w j -> p (w j)"),
             )
 
-        def passes(n):
-            k, q = ORDER[n]
-            e, c = divmod(k, 4)
-            for half in range(2):
-                bank = 2 * q + half
+        def first_matmul(n):
+            k, u = ORDER[n]
+            e, c = divmod(k, PASSES)
+            tokens = slice(T * c, T * (c + 1))
+            for i in range(2):
+                b = 2 * u + i
                 if c == 0:
-                    hb[bank] = psum.tile([P, 512], F32, tag="b%d" % bank, name="h%d_%d" % (e, bank))
-                cols = slice(512 * half, 512 * (half + 1))
+                    bank[b] = psum.tile([P, BANK], F32, tag="bank%d" % b, name="h%d_%d" % (e, b))
+                cols = slice(BANK * i, BANK * (i + 1))
                 nc.tensor.matmul_mx(
-                    out=hb[bank][:],
-                    lhsT=xq[e][:, T * c : T * (c + 1)].bitcast(FP8X4),
-                    lhsT_scale=xs[e][:, T * c : T * (c + 1)],
-                    rhs=codes[n][:, cols].bitcast(FP8X4),
-                    rhs_scale=planes[n][:, cols],
+                    out=bank[b][:],
+                    lhsT=x_words[e][:, tokens].bitcast(FP8X4),
+                    lhsT_scale=x_planes[e][:, tokens],
+                    rhs=unit_words[n][:, cols].bitcast(FP8X4),
+                    rhs_scale=unit_planes[n][:, cols],
                     start=(c == 0),
-                    stop=(c == 3),
+                    stop=(c == PASSES - 1),
                 )
 
-        def xcopy(e):
-            t = k4_pool.tile([P, 4, T, 4], BF16, tag="k4", name="xg%d" % e, align_bytes=64)
-            xg[e] = t
-            words = t[:].bitcast(F32)
-            nc.vector.tensor_copy(out=words[:, 0:2, :, :], in_=xt[(e, 0)][:].rearrange("p c u k -> p c k u"))
-            nc.scalar.copy(out=words[:, 2:4, :, :], in_=xt[(e, 1)][:].rearrange("p c u k -> p c k u"))
+        def transpose_x(x_pairs, e):
+            for i in range(2):
+                x_t[(e, i)] = psum.tile([P, 2, 2, T], F32, tag="bank%d" % (4 + 2 * e + i), name="x_t%d_%d" % (e, i))
+                for cc in range(2):
+                    first = (K_PASS // 2) * (2 * i + cc)
+                    for u in range(2):
+                        nc.tensor.transpose(
+                            x_t[(e, i)][:, cc, u, :], x_pairs[:, e, first + u : first + K_PASS // 2 : 2], ident_f32[:]
+                        )
 
-        def xquant(e):
+        def copy_x(e):
+            x_bf16[e] = small.tile([P, PASSES, T, PACK], BF16, tag="small", name="x_bf16_%d" % e, align_bytes=64)
+            pairs = x_bf16[e][:].bitcast(F32)
+            nc.vector.tensor_copy(out=pairs[:, 0:2, :, :], in_=x_t[(e, 0)][:].rearrange("p c u k -> p c k u"))
+            nc.scalar.copy(out=pairs[:, 2:4, :, :], in_=x_t[(e, 1)][:].rearrange("p c u k -> p c k u"))
+
+        def quantise_x(e):
             nc.vector.quantize_mx(
-                out=xq[e][:].bitcast(FP8X4), scales=xs[e][:], in_=xg[e][:].rearrange("p c k t -> p (c k t)")
+                out=x_words[e][:].bitcast(FP8X4),
+                scales=x_planes[e][:],
+                in_=x_bf16[e][:].rearrange("p c k t -> p (c k t)"),
             )
 
-        def gelu_a(e, i):
-            t = ga_pool.tile([P, 512], F32, tag="ga", name="ga%d_%d" % (e, i))
-            ga[i] = t
-            nc.scalar.activation(out=t[:], in_=hb[i][:], func=gelu)
+        def gelu_half(e, half):
+            for c in (2 * half, 2 * half + 1):
+                gelu_a[c] = gelu_pool.tile([P, BANK], F32, tag="gelu", name="gelu%d_%d" % (e, c))
+                nc.scalar.activation(out=gelu_a[c][:], in_=bank[c][:], func=gelu)
 
-        def gate(e, i):
-            if i == 0:
-                gp[e] = k4_pool.tile([P, 4, 4, P], BF16, tag="k4", name="gp%d" % e, align_bytes=64)
-            nc.vector.tensor_tensor(
-                out=gp[e][:, i, :, :],
-                in0=hb[4 + i][:].rearrange("k (p t) -> k t p", t=4),
-                in1=ga[i][:].rearrange("k (p t) -> k t p", t=4),
-                op=mult,
-            )
+        def gate_half(e, half):
+            if half == 0:
+                g_sorted[e] = small.tile([P, PASSES, PACK, P], BF16, tag="small", name="g_sorted%d" % e, align_bytes=64)
+            for c in (2 * half, 2 * half + 1):
+                nc.vector.tensor_tensor(
+                    out=g_sorted[e][:, c, :, :],
+                    in0=bank[PASSES + c][:].rearrange("k (p t) -> k t p", t=PACK),
+                    in1=gelu_a[c][:].rearrange("k (p t) -> k t p", t=PACK),
+                    op=mult,
+                )
+            for c in (2 * half, 2 * half + 1):
+                g_t[c] = psum.tile([P, PACK, T], BF16, tag="bank%d" % (PASSES + c), name="g_t%d_%d" % (e, c))
+                for t in range(PACK):
+                    nc.tensor.transpose(g_t[c][:, t, :], g_sorted[e][:, c, t, :], ident_bf16[:])
 
-        def g_transpose(e, i):
-            t = psum.tile([P, 4, T], BF16, tag="b%d" % (4 + i), name="pt%d_%d" % (e, i))
-            pt[i] = t
-            for tt in range(4):
-                nc.tensor.transpose(t[:, tt, :], gp[e][:, i, tt, :], ident_b[:])
+        def copy_half(e, half):
+            if half == 0:
+                g_bf16[e] = small.tile([P, PASSES, T, PACK], BF16, tag="small", name="g_bf16_%d" % e, align_bytes=64)
+            for copy, c in ((nc.vector.tensor_copy, 2 * half), (nc.scalar.copy, 2 * half + 1)):
+                copy(out=g_bf16[e][:, c, :, :], in_=g_t[c][:].rearrange("p t k -> p k t"))
 
-        def g_copy(e, i):
-            if i == 0:
-                gg_t[e] = k4_pool.tile([P, 4, T, 4], BF16, tag="k4", name="gg%d" % e, align_bytes=64)
-            src = pt[i][:].rearrange("p t k -> p k t")
-            if i % 2 == 0:
-                nc.vector.tensor_copy(out=gg_t[e][:, i, :, :], in_=src)
-            else:
-                nc.scalar.copy(out=gg_t[e][:, i, :, :], in_=src)
-
-        def g_quant(e, lo, hi):
+        def quantise_half(e, half):
+            tokens = slice(2 * T * half, 2 * T * (half + 1))
             nc.vector.quantize_mx(
-                out=gq[e][:, T * lo : T * hi].bitcast(FP8X4),
-                scales=gs[e][:, T * lo : T * hi],
-                in_=gg_t[e][:, lo:hi, :, :].rearrange("p i k t -> p (i k t)"),
+                out=g_words[e][:, tokens].bitcast(FP8X4),
+                scales=g_planes[e][:, tokens],
+                in_=g_bf16[e][:, 2 * half : 2 * half + 2, :, :].rearrange("p c k t -> p (c k t)"),
             )
 
-        def pass2(e, nb, g, bank):
-            if g == 0:
-                acc[(e, nb)] = psum.tile([P, 512], F32, tag="b%d" % bank, name="o%d_%d" % (e, nb))
-            cols = slice(512 * nb, 512 * (nb + 1))
+        def second_matmul(e, block, c):
+            if c == 0:
+                acc[(e, block)] = psum.tile(
+                    [P, BANK], F32, tag="bank%d" % OUT_BANKS[e][block], name="out%d_%d" % (e, block)
+                )
+            tokens = slice(T * c, T * (c + 1))
+            cols = slice(BANK * block, BANK * (block + 1))
             nc.tensor.matmul_mx(
-                out=acc[(e, nb)][:],
-                lhsT=gq[e][:, T * g : T * (g + 1)].bitcast(FP8X4),
-                lhsT_scale=gs[e][:, T * g : T * (g + 1)],
-                rhs=w2_words[e][:, g, cols].bitcast(FP8X4),
-                rhs_scale=w2_planes[e][4 * g : P, cols],
-                start=(g == 0),
-                stop=(g == 3),
+                out=acc[(e, block)][:],
+                lhsT=g_words[e][:, tokens].bitcast(FP8X4),
+                lhsT_scale=g_planes[e][:, tokens],
+                rhs=w2_words[e][:, c, cols].bitcast(FP8X4),
+                rhs_scale=w2_planes[e][PACK * c : P, cols],
+                start=(c == 0),
+                stop=(c == PASSES - 1),
             )
 
-        def drain(e, nb, on_vector):
-            if nb % 2 == 0:
-                ost[e] = ost_pool.tile([P, 1024], F32, tag="ost", name="ost%d_%d" % (e, nb))
-            dst = ost[e][:, 512 * (nb % 2) : 512 * (nb % 2 + 1)]
-            if on_vector:
-                nc.vector.tensor_copy(out=dst, in_=acc[(e, nb)][:])
-            else:
-                nc.scalar.copy(out=dst, in_=acc[(e, nb)][:])
-            if nb % 2 == 1:
-                nc.sync.dma_start(out=out[e][:, 512 * (nb - 1) : 512 * (nb + 1)], in_=ost[e][:])
+        def store_blocks(e, first, copies):
+            staged[e] = store_pool.tile([P, 2 * BANK], F32, tag="store", name="store%d_%d" % (e, first))
+            for i in range(2):
+                copies[i](out=staged[e][:, BANK * i : BANK * (i + 1)], in_=acc[(e, first + i)][:])
+            nc.sync.dma_start(out=out[e][:, BANK * first : BANK * (first + 2)], in_=staged[e][:])
 
         for e in range(E):
             nc.vector.memset(w2_planes[e][:].bitcast(I32), 0)
         nc.vector.memset(warm_in[:], 0.0)
         nc.scalar.activation(out=warm_out[:], in_=warm_in[:], func=gelu)
-        make_identity(nc, ident_f[:])
-        make_identity(nc, ident_b[:])
+        make_identity(nc, ident_f32[:])
+        make_identity(nc, ident_bf16[:])
 
-        alloc_chunk(0)
-        load_block(0, 0)
-        xr = stream.tile([P, E, H], BF16, tag="stream", name="xr", align_bytes=64)
-        nc.sync.dma_start(out=xr[:], in_=x.rearrange("e t h -> t e h"))
-        for b in range(1, SPLIT[0]):
-            load_block(0, b)
-            load_scales()
-        load_chunk(1)
-        load_chunk(2)
+        new_chunk(0)
+        load_piece(0, 0)
+        x_rows = stream.tile([P, E, H], BF16, tag="stream", name="x_rows", align_bytes=64)
+        nc.sync.dma_start(out=x_rows[:], in_=x.rearrange("e t h -> t e h"))
+        for piece in range(1, PIECES[0]):
+            load_piece(0, piece)
+        for i in range(1, SLOTS - 1):
+            load_stream(i)
 
         regroup(0)
-        quant(0)
-        xw = xr[:].bitcast(F32)
+        quantise(0)
         for e in range(E):
-            for half in range(2):
-                t = psum.tile([P, 2, 2, T], F32, tag="b%d" % (4 + 2 * e + half), name="xt%d_%d" % (e, half))
-                xt[(e, half)] = t
-                for cc in range(2):
-                    c = 2 * half + cc
-                    for u in range(2):
-                        nc.tensor.transpose(t[:, cc, u, :], xw[:, e, 256 * c + u : 256 * (c + 1) : 2], ident_f[:])
-        load_chunk(3)
-        xcopy(0)
-        xcopy(1)
-        xquant(0)
+            transpose_x(x_rows[:].bitcast(F32), e)
+        load_stream(SLOTS - 1)
+        copy_x(0)
+        copy_x(1)
+        quantise_x(0)
         regroup(1)
-        xquant(1)
-        passes(0)
+        quantise_x(1)
+        first_matmul(0)
 
-        for n in range(1, NU):
-            if n + 1 < NU:
+        for n in range(1, len(ORDER) + 3):
+            if n + 1 < len(ORDER):
                 regroup(n + 1)
-            if n == 16:
-                gate(0, 2)
-                gate(0, 3)
-                for i in range(4):
-                    g_transpose(0, i)
-            if n == 17:
-                for i in range(4):
-                    g_copy(0, i)
-            if n == 18:
-                g_quant(0, 0, 4)
-            if n == 30:
-                gate(1, 0)
-                gate(1, 1)
-                g_transpose(1, 0)
-                g_transpose(1, 1)
-            if n == 31:
-                g_copy(1, 0)
-                g_copy(1, 1)
-            quant(n)
-            passes(n)
-            if n == 13:
-                gelu_a(0, 0)
-                gelu_a(0, 1)
-            if n == 14:
-                gelu_a(0, 2)
-                gelu_a(0, 3)
-            if n == 15:
-                gate(0, 0)
-                gate(0, 1)
-            if n == 29:
-                gelu_a(1, 0)
-                gelu_a(1, 1)
-            if n == 30:
-                for nb in range(2):
-                    for g in range(4):
-                        pass2(0, nb, g, nb)
-
-        gelu_a(1, 2)
-        gelu_a(1, 3)
-        g_quant(1, 0, 2)
-        for nb in range(2, 4):
-            for g in range(4):
-                pass2(0, nb, g, nb + 2)
-        drain(0, 0, False)
-        drain(0, 1, False)
-        gate(1, 2)
-        gate(1, 3)
-        g_transpose(1, 2)
-        g_transpose(1, 3)
-        bank1 = [2, 3, 0, 1]
-        for g in range(2):
-            for nb in range(4):
-                pass2(1, nb, g, bank1[nb])
-        g_copy(1, 2)
-        g_copy(1, 3)
-        g_quant(1, 2, 4)
-        drain(0, 2, False)
-        drain(0, 3, False)
-        for g in range(2, 4):
-            for nb in range(4):
-                pass2(1, nb, g, bank1[nb])
-        for nb in range(4):
-            drain(1, nb, nb % 2 == 0)
+            for e in range(E):
+                for half in (1, 0):
+                    since_b = n - CLOSES[(e, 2 + half)]
+                    if since_b == 1:
+                        gate_half(e, half)
+                    if since_b == 2:
+                        copy_half(e, half)
+                    if since_b == 3:
+                        quantise_half(e, half)
+                        if (e, half) == (1, 1):
+                            store_blocks(0, 2, (nc.scalar.copy, nc.scalar.copy))
+                        if e == 1:
+                            for c in (2 * half, 2 * half + 1):
+                                for block in range(4):
+                                    second_matmul(1, block, c)
+            if n < len(ORDER):
+                quantise(n)
+                first_matmul(n)
+            if n == CLOSES[(1, 2)] + 2:
+                for block in (2, 3):
+                    for c in range(PASSES):
+                        second_matmul(0, block, c)
+            for e in range(E):
+                for half in range(2):
+                    if n == CLOSES[(e, half)] + 1:
+                        gelu_half(e, half)
+                        if (e, half) == (1, 0):
+                            for block in (0, 1):
+                                for c in range(PASSES):
+                                    second_matmul(0, block, c)
+                        if (e, half) == (1, 1):
+                            store_blocks(0, 0, (nc.scalar.copy, nc.scalar.copy))
+        for first in (0, 2):
+            store_blocks(1, first, (nc.vector.tensor_copy, nc.scalar.copy))

@@ -96,11 +96,10 @@ def tile_expert_w_kernel(tc, x, weight1, weight2_words, weight2_scales, out):
                 new_chunk(i)
                 for piece in range(PIECES[i]):
                     load_piece(i, piece)
-                if i >= PASSES:
-                    for quadrant in (2 * (i % 2), 2 * (i % 2) + 1):
-                        load_scale_rows((i - PASSES) // 2, quadrant)
             elif i < CHUNKS + E:
                 e = i - CHUNKS
+                for quadrant in range(4):
+                    load_scale_rows(e, quadrant)
                 w2_words[e] = stream.tile([P, PASSES, H], I32, tag="stream", name="w2_words%d" % e, align_bytes=64)
                 for c in range(PASSES):
                     nc.sync.dma_start(

@@ -23,7 +23,7 @@ SLOTS = 4
 FLOPS = 2 * E * T * H * 2 * F + 2 * E * T * F * H
 
 PIECES = [4, 2, 2, 2, 2, 1, 1, 1]
-VECTOR_COLS = 488
+VECTOR_COLS = 496
 ORDER = [(k, u) for k in range(CHUNKS - 1) for u in range(UNITS)] + [(CHUNKS - 1, u) for u in (0, 2, 1, 3)]
 CLOSES = dict(((e, u), ORDER.index((PASSES * e + PASSES - 1, u))) for e in range(E) for u in range(UNITS))
 OUT_BANKS = [[0, 1, 4, 5], [2, 3, 0, 1]]
@@ -118,8 +118,8 @@ def tile_expert_w_kernel(tc, x, weight1, weight2_words, weight2_scales, out):
                 (nc.scalar.copy, slice(VECTOR_COLS, UNIT)),
             ):
                 copy(
-                    out=unit_bf16[n][:, cols, :].rearrange("p (c i) j -> p c j i", i=4),
-                    in_=rows[:, :, cols].rearrange("p j (c i) -> p c j i", i=4),
+                    out=unit_bf16[n][:, cols, :].rearrange("p (c i) j -> p c j i", i=8),
+                    in_=rows[:, :, cols].rearrange("p j (c i) -> p c j i", i=8),
                 )
             if n % UNITS == UNITS - 1:
                 load_stream(n // UNITS + SLOTS)

@@ -23,7 +23,7 @@ SLOTS = 4
 FLOPS = 2 * E * T * H * 2 * F + 2 * E * T * F * H
 
 PIECES = [4, 2, 2, 2, 2, 1, 1, 1]
-VECTOR_COLS = 496
+VECTOR_COLS = 464
 ORDER = [(k, u) for k in range(CHUNKS - 1) for u in range(UNITS)] + [(CHUNKS - 1, u) for u in (0, 2, 1, 3)]
 CLOSES = dict(((e, u), ORDER.index((PASSES * e + PASSES - 1, u))) for e in range(E) for u in range(UNITS))
 OUT_BANKS = [[0, 1, 4, 5], [2, 3, 0, 1]]
@@ -113,14 +113,17 @@ def tile_expert_w_kernel(tc, x, weight1, weight2_words, weight2_scales, out):
             first = (u % per_piece) * UNIT
             rows = chunk[k][:, u // per_piece, :, first : first + UNIT]
             unit_bf16[n] = regrouped.tile([P, UNIT, PACK], BF16, tag="unit", name="unit%d" % n, align_bytes=64)
-            for copy, cols in (
-                (nc.vector.tensor_copy, slice(0, VECTOR_COLS)),
-                (nc.scalar.copy, slice(VECTOR_COLS, UNIT)),
-            ):
-                copy(
-                    out=unit_bf16[n][:, cols, :].rearrange("p (c i) j -> p c j i", i=8),
-                    in_=rows[:, :, cols].rearrange("p j (c i) -> p c j i", i=8),
-                )
+            cols = slice(0, VECTOR_COLS)
+            nc.vector.tensor_copy(
+                out=unit_bf16[n][:, cols, :].rearrange("p (c i) j -> p c j i", i=8),
+                in_=rows[:, :, cols].rearrange("p j (c i) -> p c j i", i=8),
+            )
+            cols = slice(VECTOR_COLS, UNIT)
+            nc.scalar.activation(
+                out=unit_bf16[n][:, cols, :].rearrange("p (c i) j -> p c j i", i=8),
+                in_=rows[:, :, cols].rearrange("p j (c i) -> p c j i", i=8),
+                func=mybir.ActivationFunctionType.Copy,
+            )
             if n % UNITS == UNITS - 1:
                 load_stream(n // UNITS + SLOTS)
 

@@ -23,7 +23,7 @@ SLOTS = 4
 FLOPS = 2 * E * T * H * 2 * F + 2 * E * T * F * H
 
 PIECES = [4, 2, 2, 2, 2, 1, 1, 1]
-VECTOR_COLS = 464
+VECTOR_COLS = 480
 ORDER = [(k, u) for k in range(CHUNKS - 1) for u in range(UNITS)] + [(CHUNKS - 1, u) for u in (0, 2, 1, 3)]
 CLOSES = dict(((e, u), ORDER.index((PASSES * e + PASSES - 1, u))) for e in range(E) for u in range(UNITS))
 OUT_BANKS = [[0, 1, 4, 5], [2, 3, 0, 1]]

from contextlib import ExitStack

import concourse.mybir as mybir
from concourse.masks import make_identity

FP8X4 = mybir.dt.float8_e4m3fn_x4
BF16 = mybir.dt.bfloat16
F32 = mybir.dt.float32
I32 = mybir.dt.int32
U32 = mybir.dt.uint32
U8 = mybir.dt.uint8

E, T, H, F = 2, 128, 2048, 2048
P = 128
PACK = 4
K_PASS = P * PACK
PASSES = H // K_PASS
BANK = 512
UNIT = 2 * BANK
UNITS = 2 * F // UNIT
CHUNKS = E * PASSES
SLOTS = 4
FLOPS = 2 * E * T * H * 2 * F + 2 * E * T * F * H

PIECES = [4, 2, 2, 2, 2, 1, 1, 1]
VECTOR_COLS = 480
ORDER = [(k, u) for k in range(CHUNKS - 1) for u in range(UNITS)] + [(CHUNKS - 1, u) for u in (0, 2, 1, 3)]
CLOSES = dict(((e, u), ORDER.index((PASSES * e + PASSES - 1, u))) for e in range(E) for u in range(UNITS))
OUT_BANKS = [[0, 1, 4, 5], [2, 3, 0, 1]]


def tile_expert_w_kernel(tc, x, weight1, weight2_words, weight2_scales, out):
    nc = tc.nc
    gelu = mybir.ActivationFunctionType.Gelu_apprx_tanh
    mult = mybir.AluOpType.mult
    w1_rows = weight1.rearrange("r (h c) -> (r h) c", h=2)

    with ExitStack() as ctx:
        const = ctx.enter_context(tc.tile_pool(name="const", bufs=1))
        stream = ctx.enter_context(tc.tile_pool(name="stream", bufs=SLOTS))
        regrouped = ctx.enter_context(tc.tile_pool(name="regrouped", bufs=3))
        quantised = ctx.enter_context(tc.tile_pool(name="quantised", bufs=5))
        small = ctx.enter_context(tc.tile_pool(name="small", bufs=2))
        gelu_pool = ctx.enter_context(tc.tile_pool(name="gelu", bufs=4))
        store_pool = ctx.enter_context(tc.tile_pool(name="store", bufs=4))
        psum = ctx.enter_context(tc.psum_pool(name="psum", bufs=1))
        ctx.enter_context(tc.manual_schedule())

        ident_f32 = const.tile([P, P], F32, name="ident_f32")
        ident_bf16 = const.tile([P, P], BF16, name="ident_bf16")
        warm_in = const.tile([P, 8], F32, name="warm_in")
        warm_out = const.tile([P, 8], F32, name="warm_out")
        w2_planes = [const.tile([P, H], U8, name="w2_planes%d" % e, align_bytes=64) for e in range(E)]
        x_words = [const.tile([P, PASSES * T], U32, name="x_words%d" % e, align_bytes=64) for e in range(E)]
        x_planes = [const.tile([P, PASSES * T], U8, name="x_planes%d" % e, align_bytes=64) for e in range(E)]
        g_words = [const.tile([P, PASSES * T], U32, name="g_words%d" % e, align_bytes=64) for e in range(E)]
        g_planes = [const.tile([P, PASSES * T], U8, name="g_planes%d" % e, align_bytes=64) for e in range(E)]

        chunk = {}
        w2_words = {}
        unit_bf16 = {}
        unit_words = {}
        unit_planes = {}
        bank = {}
        x_t = {}
        x_bf16 = {}
        gelu_a = {}
        g_sorted = {}
        g_t = {}
        g_bf16 = {}
        acc = {}
        staged = {}

        def load_piece(k, piece):
            width = 2 * F // PIECES[k]
            nc.sync.dma_start(
                out=chunk[k][:, piece, :, :],
                in_=w1_rows[K_PASS * k : K_PASS * (k + 1), width * piece : width * (piece + 1)].rearrange(
                    "(p j) w -> p j w", j=PACK
                ),
            )

        def load_scale_rows(e, quadrant):
            nc.sync.dma_start(
                out=w2_planes[e][32 * quadrant : 32 * quadrant + 16, :].bitcast(I32),
                in_=weight2_scales[PASSES * e : PASSES * (e + 1), 4 * quadrant : 4 * quadrant + 4, :].bitcast(I32),
            )

        def new_chunk(k):
            chunk[k] = stream.tile(
                [P, PIECES[k], PACK, 2 * F // PIECES[k]], BF16, tag="stream", name="chunk%d" % k, align_bytes=64
            )

        def load_stream(i):
            if i < CHUNKS:
                new_chunk(i)
                for piece in range(PIECES[i]):
                    load_piece(i, piece)
            elif i < CHUNKS + E:
                e = i - CHUNKS
                for quadrant in range(4):
                    load_scale_rows(e, quadrant)
                w2_words[e] = stream.tile([P, PASSES, H], I32, tag="stream", name="w2_words%d" % e, align_bytes=64)
                for c in range(PASSES):
                    nc.sync.dma_start(
                        out=w2_words[e][:, c, :],
                        in_=weight2_words[PASSES * e + c].rearrange("p n t -> p (n t)").bitcast(I32),
                    )

        def regroup(n):
            k, u = ORDER[n]
            per_piece = UNITS // PIECES[k]
            first = (u % per_piece) * UNIT
            rows = chunk[k][:, u // per_piece, :, first : first + UNIT]
            unit_bf16[n] = regrouped.tile([P, UNIT, PACK], BF16, tag="unit", name="unit%d" % n, align_bytes=64)
            cols = slice(0, VECTOR_COLS)
            nc.vector.tensor_copy(
                out=unit_bf16[n][:, cols, :].rearrange("p (c i) j -> p c j i", i=8),
                in_=rows[:, :, cols].rearrange("p j (c i) -> p c j i", i=8),
            )
            cols = slice(VECTOR_COLS, UNIT)
            nc.scalar.activation(
                out=unit_bf16[n][:, cols, :].rearrange("p (c i) j -> p c j i", i=8),
                in_=rows[:, :, cols].rearrange("p j (c i) -> p c j i", i=8),
                func=mybir.ActivationFunctionType.Copy,
            )
            if n % UNITS == UNITS - 1:
                load_stream(n // UNITS + SLOTS)

        def quantise(n):
            unit_words[n] = quantised.tile([P, UNIT], U32, tag="words", name="words%d" % n, align_bytes=64)
            unit_planes[n] = quantised.tile([P, UNIT], U8, tag="planes", name="planes%d" % n, align_bytes=64)
            nc.vector.quantize_mx(
                out=unit_words[n][:].bitcast(FP8X4),
                scales=unit_planes[n][:],
                in_=unit_bf16[n][:].rearrange("p w j -> p (w j)"),
            )

        def first_matmul(n):
            k, u = ORDER[n]
            e, c = divmod(k, PASSES)
            tokens = slice(T * c, T * (c + 1))
            for i in range(2):
                b = 2 * u + i
                if c == 0:
                    bank[b] = psum.tile([P, BANK], F32, tag="bank%d" % b, name="h%d_%d" % (e, b))
                cols = slice(BANK * i, BANK * (i + 1))
                nc.tensor.matmul_mx(
                    out=bank[b][:],
                    lhsT=x_words[e][:, tokens].bitcast(FP8X4),
                    lhsT_scale=x_planes[e][:, tokens],
                    rhs=unit_words[n][:, cols].bitcast(FP8X4),
                    rhs_scale=unit_planes[n][:, cols],
                    start=(c == 0),
                    stop=(c == PASSES - 1),
                )

        def transpose_x(x_pairs, e):
            for i in range(2):
                x_t[(e, i)] = psum.tile([P, 2, 2, T], F32, tag="bank%d" % (4 + 2 * e + i), name="x_t%d_%d" % (e, i))
                for cc in range(2):
                    first = (K_PASS // 2) * (2 * i + cc)
                    for u in range(2):
                        nc.tensor.transpose(
                            x_t[(e, i)][:, cc, u, :], x_pairs[:, e, first + u : first + K_PASS // 2 : 2], ident_f32[:]
                        )

        def copy_x(e):
            x_bf16[e] = small.tile([P, PASSES, T, PACK], BF16, tag="small", name="x_bf16_%d" % e, align_bytes=64)
            pairs = x_bf16[e][:].bitcast(F32)
            nc.vector.tensor_copy(out=pairs[:, 0:2, :, :], in_=x_t[(e, 0)][:].rearrange("p c u k -> p c k u"))
            nc.scalar.copy(out=pairs[:, 2:4, :, :], in_=x_t[(e, 1)][:].rearrange("p c u k -> p c k u"))

        def quantise_x(e):
            nc.vector.quantize_mx(
                out=x_words[e][:].bitcast(FP8X4),
                scales=x_planes[e][:],
                in_=x_bf16[e][:].rearrange("p c k t -> p (c k t)"),
            )

        def gelu_half(e, half):
            for c in (2 * half, 2 * half + 1):
                gelu_a[c] = gelu_pool.tile([P, BANK], F32, tag="gelu", name="gelu%d_%d" % (e, c))
                nc.scalar.activation(out=gelu_a[c][:], in_=bank[c][:], func=gelu)

        def gate_half(e, half):
            if half == 0:
                g_sorted[e] = small.tile([P, PASSES, PACK, P], BF16, tag="small", name="g_sorted%d" % e, align_bytes=64)
            for c in (2 * half, 2 * half + 1):
                nc.vector.tensor_tensor(
                    out=g_sorted[e][:, c, :, :],
                    in0=bank[PASSES + c][:].rearrange("k (p t) -> k t p", t=PACK),
                    in1=gelu_a[c][:].rearrange("k (p t) -> k t p", t=PACK),
                    op=mult,
                )
            for c in (2 * half, 2 * half + 1):
                g_t[c] = psum.tile([P, PACK, T], BF16, tag="bank%d" % (PASSES + c), name="g_t%d_%d" % (e, c))
                for t in range(PACK):
                    nc.tensor.transpose(g_t[c][:, t, :], g_sorted[e][:, c, t, :], ident_bf16[:])

        def copy_half(e, half):
            if half == 0:
                g_bf16[e] = small.tile([P, PASSES, T, PACK], BF16, tag="small", name="g_bf16_%d" % e, align_bytes=64)
            for copy, c in ((nc.vector.tensor_copy, 2 * half), (nc.scalar.copy, 2 * half + 1)):
                copy(out=g_bf16[e][:, c, :, :], in_=g_t[c][:].rearrange("p t k -> p k t"))

        def quantise_half(e, half):
            tokens = slice(2 * T * half, 2 * T * (half + 1))
            nc.vector.quantize_mx(
                out=g_words[e][:, tokens].bitcast(FP8X4),
                scales=g_planes[e][:, tokens],
                in_=g_bf16[e][:, 2 * half : 2 * half + 2, :, :].rearrange("p c k t -> p (c k t)"),
            )

        def second_matmul(e, block, c):
            if c == 0:
                acc[(e, block)] = psum.tile(
                    [P, BANK], F32, tag="bank%d" % OUT_BANKS[e][block], name="out%d_%d" % (e, block)
                )
            tokens = slice(T * c, T * (c + 1))
            cols = slice(BANK * block, BANK * (block + 1))
            nc.tensor.matmul_mx(
                out=acc[(e, block)][:],
                lhsT=g_words[e][:, tokens].bitcast(FP8X4),
                lhsT_scale=g_planes[e][:, tokens],
                rhs=w2_words[e][:, c, cols].bitcast(FP8X4),
                rhs_scale=w2_planes[e][PACK * c : P, cols],
                start=(c == 0),
                stop=(c == PASSES - 1),
            )

        def store_blocks(e, first, copies):
            staged[e] = store_pool.tile([P, 2 * BANK], F32, tag="store", name="store%d_%d" % (e, first))
            for i in range(2):
                copies[i](out=staged[e][:, BANK * i : BANK * (i + 1)], in_=acc[(e, first + i)][:])
            nc.sync.dma_start(out=out[e][:, BANK * first : BANK * (first + 2)], in_=staged[e][:])

        for e in range(E):
            nc.vector.memset(w2_planes[e][:].bitcast(I32), 0)
        nc.vector.memset(warm_in[:], 0.0)
        nc.scalar.activation(out=warm_out[:], in_=warm_in[:], func=gelu)
        make_identity(nc, ident_f32[:])
        make_identity(nc, ident_bf16[:])

        new_chunk(0)
        load_piece(0, 0)
        x_rows = stream.tile([P, E, H], BF16, tag="stream", name="x_rows", align_bytes=64)
        nc.sync.dma_start(out=x_rows[:], in_=x.rearrange("e t h -> t e h"))
        for piece in range(1, PIECES[0]):
            load_piece(0, piece)
        for i in range(1, SLOTS - 1):
            load_stream(i)

        regroup(0)
        quantise(0)
        for e in range(E):
            transpose_x(x_rows[:].bitcast(F32), e)
        load_stream(SLOTS - 1)
        copy_x(0)
        copy_x(1)
        quantise_x(0)
        regroup(1)
        quantise_x(1)
        first_matmul(0)

        for n in range(1, len(ORDER) + 3):
            if n + 1 < len(ORDER):
                regroup(n + 1)
            for e in range(E):
                for half in (1, 0):
                    since_b = n - CLOSES[(e, 2 + half)]
                    if since_b == 1:
                        gate_half(e, half)
                    if since_b == 2:
                        copy_half(e, half)
                    if since_b == 3:
                        quantise_half(e, half)
                        if (e, half) == (1, 1):
                            store_blocks(0, 2, (nc.scalar.copy, nc.scalar.copy))
                        if e == 1:
                            for c in (2 * half, 2 * half + 1):
                                for block in range(4):
                                    second_matmul(1, block, c)
            if n < len(ORDER):
                quantise(n)
                first_matmul(n)
            if n == CLOSES[(1, 2)] + 2:
                for block in (2, 3):
                    for c in range(PASSES):
                        second_matmul(0, block, c)
            for e in range(E):
                for half in range(2):
                    if n == CLOSES[(e, half)] + 1:
                        gelu_half(e, half)
                        if (e, half) == (1, 0):
                            for block in (0, 1):
                                for c in range(PASSES):
                                    second_matmul(0, block, c)
                        if (e, half) == (1, 1):
                            store_blocks(0, 0, (nc.scalar.copy, nc.scalar.copy))
        for first in (0, 2):
            store_blocks(1, first, (nc.vector.tensor_copy, nc.scalar.copy))
